import numpy as np
import ml_dtypes


def mxq(x, axis, fmt="e4m3"):
    dtype, down = {"e4m3": (ml_dtypes.float8_e4m3fn, 7), "e5m2": (ml_dtypes.float8_e5m2, 14)}[fmt]
    v = np.moveaxis(np.asarray(x, np.float32).astype(ml_dtypes.bfloat16).astype(np.float64), axis, -1)
    blocks = v.reshape(v.shape[:-1] + (-1, 32))
    amax = np.abs(blocks).max(-1, keepdims=True)
    byte = np.maximum(np.where(amax > 0, np.frexp(amax)[1] - 1 + 127, 0) - down, 1)
    scale = np.exp2(byte - 127.0)
    codes = (blocks / scale).astype(np.float32).astype(dtype).astype(np.float64)
    return np.moveaxis((codes * scale).reshape(v.shape), -1, axis)


WIDE = False


def mx_kscale(k):
    if not WIDE:
        return np.ones(k)
    levels = np.array([10, -10, 5, -5, 0])
    a = np.random.permutation(np.resize(levels, k // 512 * 4)).reshape(k // 512, 4)
    idx = np.arange(k)
    return np.exp2(a[idx // 512, idx % 128 // 32])


BF16 = ml_dtypes.bfloat16


def bf(x):
    return np.asarray(x, np.float32).astype(BF16)


def f64(x):
    return np.asarray(x).astype(np.float64)


B, N, I, O = 4096, 5, 512, 128
WS = 0.7 / np.sqrt(I)


def setup_inputs():
    s = mx_kscale(I)
    return {"x": bf((np.random.standard_normal((B, N, I)) * s).reshape(B, N * I)),
            "w_self": bf(np.random.standard_normal((N, O, I)) * WS / s),
            "w_parent": bf(np.random.standard_normal((N - 1, O, I)) * WS / s),
            "bias": bf(np.random.standard_normal(N * O) * 0.5)}


def reference(x, w_self, w_parent, bias):
    xq = mxq(f64(x).reshape(B, N, I).transpose(1, 0, 2), 2, "e4m3")
    y_self = xq @ mxq(f64(w_self).transpose(0, 2, 1), 1, "e4m3")
    y_par = xq[:-1] @ mxq(f64(w_parent).transpose(0, 2, 1), 1, "e4m3")
    y = np.concatenate([y_self[:1], y_self[1:] + y_par], 0)
    return y.transpose(1, 0, 2).reshape(B, N * O) + f64(bias)

@@ -1,0 +1,196 @@
+from contextlib import ExitStack
+
+import concourse.mybir as mybir
+from concourse.masks import make_identity
+
+F32 = mybir.dt.float32
+BF16 = mybir.dt.bfloat16
+U32 = mybir.dt.uint32
+U8 = mybir.dt.uint8
+FP8X4 = mybir.dt.float8_e4m3fn_x4
+ADD = mybir.AluOpType.add
+
+P = 128
+B, N, I, O = 4096, 5, 512, 128
+FLOPS = 2 * B * I * O * (2 * N - 1)
+
+CHUNKS = [4, 4, 4, 4, 4, 4, 4, 2, 2]
+XBUFS = 4
+OBUFS = 5
+LEAD = 3
+
+
+def tile_skeletonlinear_pa_t_kernel(tc, x, w_self, w_parent, bias, out):
+    nc = tc.nc
+    assert sum(CHUNKS) * P == B
+
+    chunk_base = []
+    tiles = []
+    for c, T in enumerate(CHUNKS):
+        chunk_base.append(P * len(tiles))
+        for t in range(T):
+            tiles.append((c, t))
+    n_tiles = len(tiles)
+
+    with ExitStack() as ctx:
+        const = ctx.enter_context(tc.tile_pool(name="const", bufs=1))
+        xpool = ctx.enter_context(tc.tile_pool(name="xin", bufs=XBUFS))
+        gpool = ctx.enter_context(tc.tile_pool(name="grp", bufs=3))
+        qpool = ctx.enter_context(tc.tile_pool(name="qnt", bufs=4))
+        opool = ctx.enter_context(tc.tile_pool(name="res", bufs=OBUFS))
+        pst = ctx.enter_context(tc.psum_pool(name="pst", bufs=4))
+        pso = ctx.enter_context(tc.psum_pool(name="pso", bufs=2))
+        psc = ctx.enter_context(tc.psum_pool(name="psc", bufs=2))
+        ctx.enter_context(tc.manual_schedule())
+
+        x_tiles = {}
+
+        def load(c):
+            T = CHUNKS[c]
+            xt = xpool.tile([P, T * N * I], BF16, name="xt", tag="xt")
+            r0 = chunk_base[c]
+            nc.sync.dma_start(
+                out=xt[:], in_=x[r0 : r0 + P * T, :].rearrange("(p t) c -> p (t c)", t=T)
+            )
+            x_tiles[c] = xt
+
+        ident = const.tile([P, P], F32, name="ident")
+        make_identity(nc, ident[:])
+        ones = const.tile([P, P], BF16, name="ones")
+        nc.vector.memset(ones[:], 1.0)
+        brow = const.tile([P, 768], BF16, name="brow")
+        nc.vector.memset(brow[:], 0.0)
+        nc.sync.dma_start(out=brow[0:1, 0 : N * O], in_=bias.unsqueeze(0))
+        wsb = const.tile([P, 9 * I], BF16, name="wsb")
+        nc.sync.dma_start(
+            out=wsb[:, 0 : 5 * I].rearrange("o (n i) -> o n i", n=5),
+            in_=w_self.rearrange("n o i -> o n i"),
+        )
+        nc.sync.dma_start(
+            out=wsb[:, 5 * I : 9 * I].rearrange("o (n i) -> o n i", n=4),
+            in_=w_parent.rearrange("n o i -> o n i"),
+        )
+        for c in range(min(XBUFS, len(CHUNKS))):
+            load(c)
+
+        def flip(src32, cols, dst32):
+            n = len(cols)
+            tp = pst.tile([P, 2, 256], F32, name="tp", tag="tp")
+            for u in range(2):
+                for q in range(n):
+                    c0 = cols[q] + u * P
+                    nc.tensor.transpose(tp[:, u, q * P : (q + 1) * P], src32[:, c0 : c0 + P], ident[:])
+            nc.scalar.copy(
+                out=dst32.rearrange("p (c u) -> p c u", u=2),
+                in_=tp[:, :, 0 : n * P].rearrange("p u c -> p c u"),
+            )
+
+        ww = wsb[:].bitcast(F32)
+        wg = gpool.tile([P, N * 1024], BF16, name="wg", tag="g", align_bytes=64)
+        wg32 = wg[:].bitcast(F32)
+        for i in range(5):
+            blocks = [b for b in (2 * i, 2 * i + 1) if b < 9]
+            flip(ww, [b * 256 for b in blocks], wg32[:, i * 512 : i * 512 + len(blocks) * 256])
+        wq = const.tile([P, 9 * O], U32, name="wq", align_bytes=64)
+        wsc = const.tile([P, 9 * O], U8, name="wsc", align_bytes=64)
+        nc.vector.quantize_mx(out=wq[:, 0:1024].bitcast(FP8X4), scales=wsc[:, 0:1024], in_=wg[:, 0:4096])
+        nc.vector.quantize_mx(
+            out=wq[:, 1024:1152].bitcast(FP8X4), scales=wsc[:, 1024:1152], in_=wg[:, 4096:4608]
+        )
+
+        bp0 = pso.tile([P, 512], F32, name="bp0", tag="o")
+        nc.tensor.matmul(bp0[:], lhsT=ones[:], rhs=brow[:, 0:512], start=True, stop=True)
+        bp1 = pso.tile([P, 512], F32, name="bp1", tag="o")
+        nc.tensor.matmul(bp1[:, 0:256], lhsT=ones[:], rhs=brow[:, 512:768], start=True, stop=True)
+        bias_a = const.tile([P, 512], F32, name="bias_a")
+        nc.vector.tensor_copy(out=bias_a[:], in_=bp0[:])
+        bias_c = const.tile([P, 512], F32, name="bias_c")
+        for t in range(4):
+            nc.vector.tensor_copy(out=bias_c[:, t * O : (t + 1) * O], in_=bp1[:, 0:O])
+
+        g_tiles = {}
+        q_tiles = {}
+        c_tiles = {}
+        o_tiles = {}
+
+        def transposes(h):
+            k, part = divmod(h, 2)
+            c, t0 = tiles[2 * k]
+            xw = x_tiles[c][:].bitcast(F32)
+            if part == 0:
+                g_tiles[k] = gpool.tile([P, N * 1024], BF16, name="g", tag="g", align_bytes=64)
+            g32 = g_tiles[k][:].bitcast(F32)
+            for j in ((0, 1) if part == 0 else (2, 3, 4)):
+                flip(
+                    xw,
+                    [(t0 + q) * (N * 256) + j * 256 for q in range(2)],
+                    g32[:, j * 512 : (j + 1) * 512],
+                )
+            if part == 1 and t0 + 2 == CHUNKS[c] and c + XBUFS < len(CHUNKS):
+                load(c + XBUFS)
+
+        def quantise(h):
+            k, part = divmod(h, 2)
+            g = g_tiles[k]
+            if part == 0:
+                xq = qpool.tile([P, N * 256], U32, name="xq", tag="xq", align_bytes=64)
+                xs = qpool.tile([P, N * 256], U8, name="xs", tag="xs", align_bytes=64)
+                q_tiles[k] = (xq, xs)
+                spans = [(0, 512)]
+            else:
+                xq, xs = q_tiles[k]
+                spans = [(512, 1024), (1024, 1280)]
+            for a, b in spans:
+                nc.vector.quantize_mx(
+                    out=xq[:, a:b].bitcast(FP8X4), scales=xs[:, a:b], in_=g[:, 4 * a : 4 * b]
+                )
+
+        def mx(acc, xq, xs, col, b, start, stop):
+            nc.tensor.matmul_mx(
+                out=acc,
+                lhsT=xq[:, col : col + P].bitcast(FP8X4),
+                lhsT_scale=xs[:, col : col + P],
+                rhs=wq[:, b * O : (b + 1) * O].bitcast(FP8X4),
+                rhs_scale=wsc[:, b * O : (b + 1) * O],
+                start=start,
+                stop=stop,
+            )
+
+        def passes(s):
+            c, t = tiles[s]
+            T = CHUNKS[c]
+            xq, xs = q_tiles[s // 2]
+            q = s % 2
+            acc = pso.tile([P, 512], F32, name="acc", tag="o")
+            if t == 0:
+                c_tiles[c] = psc.tile([P, 512], F32, name="acc4", tag="c")
+                o_tiles[c] = opool.tile([P, T * N * O], F32, name="res", tag="res")
+            acc4 = c_tiles[c]
+            res = o_tiles[c]
+            for j in range(N):
+                dst = acc[:, j * O : (j + 1) * O] if j < 4 else acc4[:, t * O : (t + 1) * O]
+                if j > 0:
+                    mx(dst, xq, xs, (j - 1) * 256 + q * P, 5 + j - 1, True, False)
+                mx(dst, xq, xs, j * 256 + q * P, j, j == 0, True)
+            nc.vector.tensor_tensor(
+                out=res[:, t * N * O : t * N * O + 512], in0=acc[:], in1=bias_a[:], op=ADD
+            )
+            if t == T - 1:
+                nc.vector.tensor_tensor(
+                    out=res[:].rearrange("p (t c) -> p t c", t=T)[:, :, 512:640],
+                    in0=acc4[:, 0 : T * O].rearrange("p (t c) -> p t c", t=T),
+                    in1=bias_c[:, 0 : T * O].rearrange("p (t c) -> p t c", t=T),
+                    op=ADD,
+                )
+                r0 = chunk_base[c]
+                nc.sync.dma_start(
+                    out=out[r0 : r0 + P * T, :].rearrange("(p t) c -> p (t c)", t=T), in_=res[:]
+                )
+
+        for s in range(-LEAD, n_tiles):
+            if s + LEAD < n_tiles:
+                transposes(s + LEAD)
+            if 0 <= s + LEAD - 1 < n_tiles:
+                quantise(s + LEAD - 1)
+            if s >= 0:
+                passes(s)

@@ -17,7 +17,6 @@ FLOPS = 2 * B * I * O * (2 * N - 1)
 CHUNKS = [4, 4, 4, 4, 4, 4, 4, 2, 2]
 XBUFS = 4
 OBUFS = 5
-LEAD = 3
 
 
 def tile_skeletonlinear_pa_t_kernel(tc, x, w_self, w_parent, bias, out):
@@ -112,35 +111,28 @@ def tile_skeletonlinear_pa_t_kernel(tc, x, w_self, w_parent, bias, out):
         q_tiles = {}
         c_tiles = {}
         o_tiles = {}
+        a_tiles = {}
 
-        def transposes(h):
-            k, part = divmod(h, 2)
+        def transposes(k):
             c, t0 = tiles[2 * k]
             xw = x_tiles[c][:].bitcast(F32)
-            if part == 0:
-                g_tiles[k] = gpool.tile([P, N * 1024], BF16, name="g", tag="g", align_bytes=64)
+            g_tiles[k] = gpool.tile([P, N * 1024], BF16, name="g", tag="g", align_bytes=64)
             g32 = g_tiles[k][:].bitcast(F32)
-            for j in ((0, 1) if part == 0 else (2, 3, 4)):
+            for j in range(N):
                 flip(
                     xw,
                     [(t0 + q) * (N * 256) + j * 256 for q in range(2)],
                     g32[:, j * 512 : (j + 1) * 512],
                 )
-            if part == 1 and t0 + 2 == CHUNKS[c] and c + XBUFS < len(CHUNKS):
+            if t0 + 2 == CHUNKS[c] and c + XBUFS < len(CHUNKS):
                 load(c + XBUFS)
 
-        def quantise(h):
-            k, part = divmod(h, 2)
+        def quantise(k):
             g = g_tiles[k]
-            if part == 0:
-                xq = qpool.tile([P, N * 256], U32, name="xq", tag="xq", align_bytes=64)
-                xs = qpool.tile([P, N * 256], U8, name="xs", tag="xs", align_bytes=64)
-                q_tiles[k] = (xq, xs)
-                spans = [(0, 512)]
-            else:
-                xq, xs = q_tiles[k]
-                spans = [(512, 1024), (1024, 1280)]
-            for a, b in spans:
+            xq = qpool.tile([P, N * 256], U32, name="xq", tag="xq", align_bytes=64)
+            xs = qpool.tile([P, N * 256], U8, name="xs", tag="xs", align_bytes=64)
+            q_tiles[k] = (xq, xs)
+            for a, b in ((0, 512), (512, 1024), (1024, 1280)):
                 nc.vector.quantize_mx(
                     out=xq[:, a:b].bitcast(FP8X4), scales=xs[:, a:b], in_=g[:, 4 * a : 4 * b]
                 )
@@ -156,41 +148,50 @@ def tile_skeletonlinear_pa_t_kernel(tc, x, w_self, w_parent, bias, out):
                 stop=stop,
             )
 
-        def passes(s):
-            c, t = tiles[s]
-            T = CHUNKS[c]
-            xq, xs = q_tiles[s // 2]
-            q = s % 2
-            acc = pso.tile([P, 512], F32, name="acc", tag="o")
-            if t == 0:
-                c_tiles[c] = psc.tile([P, 512], F32, name="acc4", tag="c")
-                o_tiles[c] = opool.tile([P, T * N * O], F32, name="res", tag="res")
-            acc4 = c_tiles[c]
-            res = o_tiles[c]
-            for j in range(N):
-                dst = acc[:, j * O : (j + 1) * O] if j < 4 else acc4[:, t * O : (t + 1) * O]
-                if j > 0:
-                    mx(dst, xq, xs, (j - 1) * 256 + q * P, 5 + j - 1, True, False)
-                mx(dst, xq, xs, j * 256 + q * P, j, j == 0, True)
-            nc.vector.tensor_tensor(
-                out=res[:, t * N * O : t * N * O + 512], in0=acc[:], in1=bias_a[:], op=ADD
-            )
-            if t == T - 1:
-                nc.vector.tensor_tensor(
-                    out=res[:].rearrange("p (t c) -> p t c", t=T)[:, :, 512:640],
-                    in0=acc4[:, 0 : T * O].rearrange("p (t c) -> p t c", t=T),
-                    in1=bias_c[:, 0 : T * O].rearrange("p (t c) -> p t c", t=T),
-                    op=ADD,
-                )
-                r0 = chunk_base[c]
-                nc.sync.dma_start(
-                    out=out[r0 : r0 + P * T, :].rearrange("(p t) c -> p (t c)", t=T), in_=res[:]
-                )
+        def passes(k):
+            xq, xs = q_tiles[k]
+            for q in range(2):
+                c, t = tiles[2 * k + q]
+                acc = pso.tile([P, 512], F32, name="acc", tag="o")
+                a_tiles[2 * k + q] = acc
+                if t == 0:
+                    c_tiles[c] = psc.tile([P, 512], F32, name="acc4", tag="c")
+                acc4 = c_tiles[c]
+                for j in range(N):
+                    dst = acc[:, j * O : (j + 1) * O] if j < 4 else acc4[:, t * O : (t + 1) * O]
+                    if j > 0:
+                        mx(dst, xq, xs, (j - 1) * 256 + q * P, 5 + j - 1, True, False)
+                    mx(dst, xq, xs, j * 256 + q * P, j, j == 0, True)
 
-        for s in range(-LEAD, n_tiles):
-            if s + LEAD < n_tiles:
-                transposes(s + LEAD)
-            if 0 <= s + LEAD - 1 < n_tiles:
-                quantise(s + LEAD - 1)
-            if s >= 0:
-                passes(s)
+        def finish(k):
+            for q in range(2):
+                c, t = tiles[2 * k + q]
+                T = CHUNKS[c]
+                if t == 0:
+                    o_tiles[c] = opool.tile([P, T * N * O], F32, name="res", tag="res")
+                res = o_tiles[c]
+                nc.vector.tensor_tensor(
+                    out=res[:, t * N * O : t * N * O + 512], in0=a_tiles[2 * k + q][:], in1=bias_a[:], op=ADD
+                )
+                if t == T - 1:
+                    nc.vector.tensor_tensor(
+                        out=res[:].rearrange("p (t c) -> p t c", t=T)[:, :, 512:640],
+                        in0=c_tiles[c][:, 0 : T * O].rearrange("p (t c) -> p t c", t=T),
+                        in1=bias_c[:, 0 : T * O].rearrange("p (t c) -> p t c", t=T),
+                        op=ADD,
+                    )
+                    r0 = chunk_base[c]
+                    nc.sync.dma_start(
+                        out=out[r0 : r0 + P * T, :].rearrange("(p t) c -> p (t c)", t=T), in_=res[:]
+                    )
+
+        n_pairs = n_tiles // 2
+        for k in range(-1, n_pairs + 1):
+            if k + 1 < n_pairs:
+                transposes(k + 1)
+            if k >= 1:
+                finish(k - 1)
+            if k + 1 < n_pairs:
+                quantise(k + 1)
+            if 0 <= k < n_pairs:
+                passes(k)

@@ -14,9 +14,10 @@ P = 128
 B, N, I, O = 4096, 5, 512, 128
 FLOPS = 2 * B * I * O * (2 * N - 1)
 
-CHUNKS = [4, 4, 4, 4, 4, 4, 4, 2, 2]
-XBUFS = 4
-OBUFS = 5
+CHUNKS = [2, 2, 2, 2, 4, 4, 4, 4, 4, 2, 2]
+XBUFS = {2: 4, 4: 3}
+OBUFS = {2: 4, 4: 3}
+LEAD = 3
 
 
 def tile_skeletonlinear_pa_t_kernel(tc, x, w_self, w_parent, bias, out):
@@ -33,33 +34,32 @@ def tile_skeletonlinear_pa_t_kernel(tc, x, w_self, w_parent, bias, out):
 
     with ExitStack() as ctx:
         const = ctx.enter_context(tc.tile_pool(name="const", bufs=1))
-        xpool = ctx.enter_context(tc.tile_pool(name="xin", bufs=XBUFS))
+        xpool = ctx.enter_context(tc.tile_pool(name="xin", bufs=1))
         gpool = ctx.enter_context(tc.tile_pool(name="grp", bufs=3))
-        qpool = ctx.enter_context(tc.tile_pool(name="qnt", bufs=4))
-        opool = ctx.enter_context(tc.tile_pool(name="res", bufs=OBUFS))
+        qpool = ctx.enter_context(tc.tile_pool(name="qnt", bufs=3))
+        opool = ctx.enter_context(tc.tile_pool(name="res", bufs=1))
         pst = ctx.enter_context(tc.psum_pool(name="pst", bufs=4))
         pso = ctx.enter_context(tc.psum_pool(name="pso", bufs=2))
         psc = ctx.enter_context(tc.psum_pool(name="psc", bufs=2))
         ctx.enter_context(tc.manual_schedule())
 
         x_tiles = {}
+        x_free = dict(XBUFS)
+        state = {"next_load": 0}
 
-        def load(c):
-            T = CHUNKS[c]
-            xt = xpool.tile([P, T * N * I], BF16, name="xt", tag="xt")
-            r0 = chunk_base[c]
-            nc.sync.dma_start(
-                out=xt[:], in_=x[r0 : r0 + P * T, :].rearrange("(p t) c -> p (t c)", t=T)
-            )
-            x_tiles[c] = xt
+        def issue_loads():
+            while state["next_load"] < len(CHUNKS) and x_free[CHUNKS[state["next_load"]]] > 0:
+                c = state["next_load"]
+                T = CHUNKS[c]
+                state["next_load"] = c + 1
+                x_free[T] = x_free[T] - 1
+                xt = xpool.tile([P, T * N * I], BF16, name="xt%d" % T, tag="xt%d" % T, bufs=XBUFS[T])
+                r0 = chunk_base[c]
+                nc.sync.dma_start(
+                    out=xt[:], in_=x[r0 : r0 + P * T, :].rearrange("(p t) c -> p (t c)", t=T)
+                )
+                x_tiles[c] = xt
 
-        ident = const.tile([P, P], F32, name="ident")
-        make_identity(nc, ident[:])
-        ones = const.tile([P, P], BF16, name="ones")
-        nc.vector.memset(ones[:], 1.0)
-        brow = const.tile([P, 768], BF16, name="brow")
-        nc.vector.memset(brow[:], 0.0)
-        nc.sync.dma_start(out=brow[0:1, 0 : N * O], in_=bias.unsqueeze(0))
         wsb = const.tile([P, 9 * I], BF16, name="wsb")
         nc.sync.dma_start(
             out=wsb[:, 0 : 5 * I].rearrange("o (n i) -> o n i", n=5),
@@ -69,8 +69,14 @@ def tile_skeletonlinear_pa_t_kernel(tc, x, w_self, w_parent, bias, out):
             out=wsb[:, 5 * I : 9 * I].rearrange("o (n i) -> o n i", n=4),
             in_=w_parent.rearrange("n o i -> o n i"),
         )
-        for c in range(min(XBUFS, len(CHUNKS))):
-            load(c)
+        issue_loads()
+        ident = const.tile([P, P], F32, name="ident")
+        make_identity(nc, ident[:])
+        brow = const.tile([P, 768], BF16, name="brow")
+        nc.vector.memset(brow[:], 0.0)
+        nc.scalar.dma_start(out=brow[0:1, 0 : N * O], in_=bias.unsqueeze(0))
+        ones = const.tile([P, P], BF16, name="ones")
+        nc.vector.memset(ones[:], 1.0)
 
         def flip(src32, cols, dst32):
             n = len(cols)
@@ -111,28 +117,36 @@ def tile_skeletonlinear_pa_t_kernel(tc, x, w_self, w_parent, bias, out):
         q_tiles = {}
         c_tiles = {}
         o_tiles = {}
-        a_tiles = {}
 
-        def transposes(k):
+        def transposes(h):
+            k, part = divmod(h, 2)
             c, t0 = tiles[2 * k]
             xw = x_tiles[c][:].bitcast(F32)
-            g_tiles[k] = gpool.tile([P, N * 1024], BF16, name="g", tag="g", align_bytes=64)
+            if part == 0:
+                g_tiles[k] = gpool.tile([P, N * 1024], BF16, name="g", tag="g", align_bytes=64)
             g32 = g_tiles[k][:].bitcast(F32)
-            for j in range(N):
+            for j in ((0, 1) if part == 0 else (2, 3, 4)):
                 flip(
                     xw,
                     [(t0 + q) * (N * 256) + j * 256 for q in range(2)],
                     g32[:, j * 512 : (j + 1) * 512],
                 )
-            if t0 + 2 == CHUNKS[c] and c + XBUFS < len(CHUNKS):
-                load(c + XBUFS)
+            if part == 1 and t0 + 2 == CHUNKS[c]:
+                x_free[CHUNKS[c]] = x_free[CHUNKS[c]] + 1
+                issue_loads()
 
-        def quantise(k):
+        def quantise(h):
+            k, part = divmod(h, 2)
             g = g_tiles[k]
-            xq = qpool.tile([P, N * 256], U32, name="xq", tag="xq", align_bytes=64)
-            xs = qpool.tile([P, N * 256], U8, name="xs", tag="xs", align_bytes=64)
-            q_tiles[k] = (xq, xs)
-            for a, b in ((0, 512), (512, 1024), (1024, 1280)):
+            if part == 0:
+                xq = qpool.tile([P, N * 256], U32, name="xq", tag="xq", align_bytes=64)
+                xs = qpool.tile([P, N * 256], U8, name="xs", tag="xs", align_bytes=64)
+                q_tiles[k] = (xq, xs)
+                spans = [(0, 512)]
+            else:
+                xq, xs = q_tiles[k]
+                spans = [(512, 1024), (1024, 1280)]
+            for a, b in spans:
                 nc.vector.quantize_mx(
                     out=xq[:, a:b].bitcast(FP8X4), scales=xs[:, a:b], in_=g[:, 4 * a : 4 * b]
                 )
@@ -148,50 +162,41 @@ def tile_skeletonlinear_pa_t_kernel(tc, x, w_self, w_parent, bias, out):
                 stop=stop,
             )
 
-        def passes(k):
-            xq, xs = q_tiles[k]
-            for q in range(2):
-                c, t = tiles[2 * k + q]
-                acc = pso.tile([P, 512], F32, name="acc", tag="o")
-                a_tiles[2 * k + q] = acc
-                if t == 0:
-                    c_tiles[c] = psc.tile([P, 512], F32, name="acc4", tag="c")
-                acc4 = c_tiles[c]
-                for j in range(N):
-                    dst = acc[:, j * O : (j + 1) * O] if j < 4 else acc4[:, t * O : (t + 1) * O]
-                    if j > 0:
-                        mx(dst, xq, xs, (j - 1) * 256 + q * P, 5 + j - 1, True, False)
-                    mx(dst, xq, xs, j * 256 + q * P, j, j == 0, True)
-
-        def finish(k):
-            for q in range(2):
-                c, t = tiles[2 * k + q]
-                T = CHUNKS[c]
-                if t == 0:
-                    o_tiles[c] = opool.tile([P, T * N * O], F32, name="res", tag="res")
-                res = o_tiles[c]
+        def passes(s):
+            c, t = tiles[s]
+            T = CHUNKS[c]
+            xq, xs = q_tiles[s // 2]
+            q = s % 2
+            acc = pso.tile([P, 512], F32, name="acc", tag="o")
+            if t == 0:
+                c_tiles[c] = psc.tile([P, 512], F32, name="acc4", tag="c")
+                o_tiles[c] = opool.tile([P, T * N * O], F32, name="res%d" % T, tag="res%d" % T, bufs=OBUFS[T])
+            acc4 = c_tiles[c]
+            res = o_tiles[c]
+            for j in range(N):
+                dst = acc[:, j * O : (j + 1) * O] if j < 4 else acc4[:, t * O : (t + 1) * O]
+                if j > 0:
+                    mx(dst, xq, xs, (j - 1) * 256 + q * P, 5 + j - 1, True, False)
+                mx(dst, xq, xs, j * 256 + q * P, j, j == 0, True)
+            nc.vector.tensor_tensor(
+                out=res[:, t * N * O : t * N * O + 512], in0=acc[:], in1=bias_a[:], op=ADD
+            )
+            if t == T - 1:
                 nc.vector.tensor_tensor(
-                    out=res[:, t * N * O : t * N * O + 512], in0=a_tiles[2 * k + q][:], in1=bias_a[:], op=ADD
+                    out=res[:].rearrange("p (t c) -> p t c", t=T)[:, :, 512:640],
+                    in0=acc4[:, 0 : T * O].rearrange("p (t c) -> p t c", t=T),
+                    in1=bias_c[:, 0 : T * O].rearrange("p (t c) -> p t c", t=T),
+                    op=ADD,
                 )
-                if t == T - 1:
-                    nc.vector.tensor_tensor(
-                        out=res[:].rearrange("p (t c) -> p t c", t=T)[:, :, 512:640],
-                        in0=c_tiles[c][:, 0 : T * O].rearrange("p (t c) -> p t c", t=T),
-                        in1=bias_c[:, 0 : T * O].rearrange("p (t c) -> p t c", t=T),
-                        op=ADD,
-                    )
-                    r0 = chunk_base[c]
-                    nc.sync.dma_start(
-                        out=out[r0 : r0 + P * T, :].rearrange("(p t) c -> p (t c)", t=T), in_=res[:]
-                    )
+                r0 = chunk_base[c]
+                nc.sync.dma_start(
+                    out=out[r0 : r0 + P * T, :].rearrange("(p t) c -> p (t c)", t=T), in_=res[:]
+                )
 
-        n_pairs = n_tiles // 2
-        for k in range(-1, n_pairs + 1):
-            if k + 1 < n_pairs:
-                transposes(k + 1)
-            if k >= 1:
-                finish(k - 1)
-            if k + 1 < n_pairs:
-                quantise(k + 1)
-            if 0 <= k < n_pairs:
-                passes(k)
+        for s in range(-LEAD, n_tiles):
+            if s + LEAD < n_tiles:
+                transposes(s + LEAD)
+            if 0 <= s + LEAD - 1 < n_tiles:
+                quantise(s + LEAD - 1)
+            if s >= 0:
+                passes(s)

@@ -14,9 +14,9 @@ P = 128
 B, N, I, O = 4096, 5, 512, 128
 FLOPS = 2 * B * I * O * (2 * N - 1)
 
-CHUNKS = [2, 2, 2, 2, 4, 4, 4, 4, 4, 2, 2]
-XBUFS = {2: 4, 4: 3}
-OBUFS = {2: 4, 4: 3}
+CHUNKS = [2, 2, 4, 4, 4, 4, 4, 4, 2, 2]
+XBUFS = 4
+OBUFS = 5
 LEAD = 3
 
 
@@ -34,32 +34,33 @@ def tile_skeletonlinear_pa_t_kernel(tc, x, w_self, w_parent, bias, out):
 
     with ExitStack() as ctx:
         const = ctx.enter_context(tc.tile_pool(name="const", bufs=1))
-        xpool = ctx.enter_context(tc.tile_pool(name="xin", bufs=1))
+        xpool = ctx.enter_context(tc.tile_pool(name="xin", bufs=XBUFS))
         gpool = ctx.enter_context(tc.tile_pool(name="grp", bufs=3))
-        qpool = ctx.enter_context(tc.tile_pool(name="qnt", bufs=3))
-        opool = ctx.enter_context(tc.tile_pool(name="res", bufs=1))
+        qpool = ctx.enter_context(tc.tile_pool(name="qnt", bufs=4))
+        opool = ctx.enter_context(tc.tile_pool(name="res", bufs=OBUFS))
         pst = ctx.enter_context(tc.psum_pool(name="pst", bufs=4))
         pso = ctx.enter_context(tc.psum_pool(name="pso", bufs=2))
         psc = ctx.enter_context(tc.psum_pool(name="psc", bufs=2))
         ctx.enter_context(tc.manual_schedule())
 
         x_tiles = {}
-        x_free = dict(XBUFS)
-        state = {"next_load": 0}
 
-        def issue_loads():
-            while state["next_load"] < len(CHUNKS) and x_free[CHUNKS[state["next_load"]]] > 0:
-                c = state["next_load"]
-                T = CHUNKS[c]
-                state["next_load"] = c + 1
-                x_free[T] = x_free[T] - 1
-                xt = xpool.tile([P, T * N * I], BF16, name="xt%d" % T, tag="xt%d" % T, bufs=XBUFS[T])
-                r0 = chunk_base[c]
-                nc.sync.dma_start(
-                    out=xt[:], in_=x[r0 : r0 + P * T, :].rearrange("(p t) c -> p (t c)", t=T)
-                )
-                x_tiles[c] = xt
+        def load(c):
+            T = CHUNKS[c]
+            xt = xpool.tile([P, T * N * I], BF16, name="xt", tag="xt")
+            r0 = chunk_base[c]
+            nc.sync.dma_start(
+                out=xt[:], in_=x[r0 : r0 + P * T, :].rearrange("(p t) c -> p (t c)", t=T)
+            )
+            x_tiles[c] = xt
 
+        ident = const.tile([P, P], F32, name="ident")
+        make_identity(nc, ident[:])
+        ones = const.tile([P, P], BF16, name="ones")
+        nc.vector.memset(ones[:], 1.0)
+        brow = const.tile([P, 768], BF16, name="brow")
+        nc.vector.memset(brow[:], 0.0)
+        nc.sync.dma_start(out=brow[0:1, 0 : N * O], in_=bias.unsqueeze(0))
         wsb = const.tile([P, 9 * I], BF16, name="wsb")
         nc.sync.dma_start(
             out=wsb[:, 0 : 5 * I].rearrange("o (n i) -> o n i", n=5),
@@ -69,14 +70,8 @@ def tile_skeletonlinear_pa_t_kernel(tc, x, w_self, w_parent, bias, out):
             out=wsb[:, 5 * I : 9 * I].rearrange("o (n i) -> o n i", n=4),
             in_=w_parent.rearrange("n o i -> o n i"),
         )
-        issue_loads()
-        ident = const.tile([P, P], F32, name="ident")
-        make_identity(nc, ident[:])
-        brow = const.tile([P, 768], BF16, name="brow")
-        nc.vector.memset(brow[:], 0.0)
-        nc.scalar.dma_start(out=brow[0:1, 0 : N * O], in_=bias.unsqueeze(0))
-        ones = const.tile([P, P], BF16, name="ones")
-        nc.vector.memset(ones[:], 1.0)
+        for c in range(min(XBUFS, len(CHUNKS))):
+            load(c)
 
         def flip(src32, cols, dst32):
             n = len(cols)
@@ -131,9 +126,8 @@ def tile_skeletonlinear_pa_t_kernel(tc, x, w_self, w_parent, bias, out):
                     [(t0 + q) * (N * 256) + j * 256 for q in range(2)],
                     g32[:, j * 512 : (j + 1) * 512],
                 )
-            if part == 1 and t0 + 2 == CHUNKS[c]:
-                x_free[CHUNKS[c]] = x_free[CHUNKS[c]] + 1
-                issue_loads()
+            if part == 1 and t0 + 2 == CHUNKS[c] and c + XBUFS < len(CHUNKS):
+                load(c + XBUFS)
 
         def quantise(h):
             k, part = divmod(h, 2)
@@ -170,7 +164,7 @@ def tile_skeletonlinear_pa_t_kernel(tc, x, w_self, w_parent, bias, out):
             acc = pso.tile([P, 512], F32, name="acc", tag="o")
             if t == 0:
                 c_tiles[c] = psc.tile([P, 512], F32, name="acc4", tag="c")
-                o_tiles[c] = opool.tile([P, T * N * O], F32, name="res%d" % T, tag="res%d" % T, bufs=OBUFS[T])
+                o_tiles[c] = opool.tile([P, T * N * O], F32, name="res", tag="res")
             acc4 = c_tiles[c]
             res = o_tiles[c]
             for j in range(N):

from contextlib import ExitStack

import concourse.mybir as mybir
from concourse.masks import make_identity

F32 = mybir.dt.float32
BF16 = mybir.dt.bfloat16
U32 = mybir.dt.uint32
U8 = mybir.dt.uint8
FP8X4 = mybir.dt.float8_e4m3fn_x4
ADD = mybir.AluOpType.add

P = 128
B, N, I, O = 4096, 5, 512, 128
FLOPS = 2 * B * I * O * (2 * N - 1)

CHUNKS = [2, 2, 4, 4, 4, 4, 4, 4, 2, 2]
XBUFS = 4
OBUFS = 5
LEAD = 3


def tile_skeletonlinear_pa_t_kernel(tc, x, w_self, w_parent, bias, out):
    nc = tc.nc
    assert sum(CHUNKS) * P == B

    chunk_base = []
    tiles = []
    for c, T in enumerate(CHUNKS):
        chunk_base.append(P * len(tiles))
        for t in range(T):
            tiles.append((c, t))
    n_tiles = len(tiles)

    with ExitStack() as ctx:
        const = ctx.enter_context(tc.tile_pool(name="const", bufs=1))
        xpool = ctx.enter_context(tc.tile_pool(name="xin", bufs=XBUFS))
        gpool = ctx.enter_context(tc.tile_pool(name="grp", bufs=3))
        qpool = ctx.enter_context(tc.tile_pool(name="qnt", bufs=4))
        opool = ctx.enter_context(tc.tile_pool(name="res", bufs=OBUFS))
        pst = ctx.enter_context(tc.psum_pool(name="pst", bufs=4))
        pso = ctx.enter_context(tc.psum_pool(name="pso", bufs=2))
        psc = ctx.enter_context(tc.psum_pool(name="psc", bufs=2))
        ctx.enter_context(tc.manual_schedule())

        x_tiles = {}

        def load(c):
            T = CHUNKS[c]
            xt = xpool.tile([P, T * N * I], BF16, name="xt", tag="xt")
            r0 = chunk_base[c]
            nc.sync.dma_start(
                out=xt[:], in_=x[r0 : r0 + P * T, :].rearrange("(p t) c -> p (t c)", t=T)
            )
            x_tiles[c] = xt

        ident = const.tile([P, P], F32, name="ident")
        make_identity(nc, ident[:])
        ones = const.tile([P, P], BF16, name="ones")
        nc.vector.memset(ones[:], 1.0)
        brow = const.tile([P, 768], BF16, name="brow")
        nc.vector.memset(brow[:], 0.0)
        nc.sync.dma_start(out=brow[0:1, 0 : N * O], in_=bias.unsqueeze(0))
        wsb = const.tile([P, 9 * I], BF16, name="wsb")
        nc.sync.dma_start(
            out=wsb[:, 0 : 5 * I].rearrange("o (n i) -> o n i", n=5),
            in_=w_self.rearrange("n o i -> o n i"),
        )
        nc.sync.dma_start(
            out=wsb[:, 5 * I : 9 * I].rearrange("o (n i) -> o n i", n=4),
            in_=w_parent.rearrange("n o i -> o n i"),
        )
        for c in range(min(XBUFS, len(CHUNKS))):
            load(c)

        def flip(src32, cols, dst32):
            n = len(cols)
            tp = pst.tile([P, 2, 256], F32, name="tp", tag="tp")
            for u in range(2):
                for q in range(n):
                    c0 = cols[q] + u * P
                    nc.tensor.transpose(tp[:, u, q * P : (q + 1) * P], src32[:, c0 : c0 + P], ident[:])
            nc.scalar.copy(
                out=dst32.rearrange("p (c u) -> p c u", u=2),
                in_=tp[:, :, 0 : n * P].rearrange("p u c -> p c u"),
            )

        ww = wsb[:].bitcast(F32)
        wg = gpool.tile([P, N * 1024], BF16, name="wg", tag="g", align_bytes=64)
        wg32 = wg[:].bitcast(F32)
        for i in range(5):
            blocks = [b for b in (2 * i, 2 * i + 1) if b < 9]
            flip(ww, [b * 256 for b in blocks], wg32[:, i * 512 : i * 512 + len(blocks) * 256])
        wq = const.tile([P, 9 * O], U32, name="wq", align_bytes=64)
        wsc = const.tile([P, 9 * O], U8, name="wsc", align_bytes=64)
        nc.vector.quantize_mx(out=wq[:, 0:1024].bitcast(FP8X4), scales=wsc[:, 0:1024], in_=wg[:, 0:4096])
        nc.vector.quantize_mx(
            out=wq[:, 1024:1152].bitcast(FP8X4), scales=wsc[:, 1024:1152], in_=wg[:, 4096:4608]
        )

        bp0 = pso.tile([P, 512], F32, name="bp0", tag="o")
        nc.tensor.matmul(bp0[:], lhsT=ones[:], rhs=brow[:, 0:512], start=True, stop=True)
        bp1 = pso.tile([P, 512], F32, name="bp1", tag="o")
        nc.tensor.matmul(bp1[:, 0:256], lhsT=ones[:], rhs=brow[:, 512:768], start=True, stop=True)
        bias_a = const.tile([P, 512], F32, name="bias_a")
        nc.vector.tensor_copy(out=bias_a[:], in_=bp0[:])
        bias_c = const.tile([P, 512], F32, name="bias_c")
        for t in range(4):
            nc.vector.tensor_copy(out=bias_c[:, t * O : (t + 1) * O], in_=bp1[:, 0:O])

        g_tiles = {}
        q_tiles = {}
        c_tiles = {}
        o_tiles = {}

        def transposes(h):
            k, part = divmod(h, 2)
            c, t0 = tiles[2 * k]
            xw = x_tiles[c][:].bitcast(F32)
            if part == 0:
                g_tiles[k] = gpool.tile([P, N * 1024], BF16, name="g", tag="g", align_bytes=64)
            g32 = g_tiles[k][:].bitcast(F32)
            for j in ((0, 1) if part == 0 else (2, 3, 4)):
                flip(
                    xw,
                    [(t0 + q) * (N * 256) + j * 256 for q in range(2)],
                    g32[:, j * 512 : (j + 1) * 512],
                )
            if part == 1 and t0 + 2 == CHUNKS[c] and c + XBUFS < len(CHUNKS):
                load(c + XBUFS)

        def quantise(h):
            k, part = divmod(h, 2)
            g = g_tiles[k]
            if part == 0:
                xq = qpool.tile([P, N * 256], U32, name="xq", tag="xq", align_bytes=64)
                xs = qpool.tile([P, N * 256], U8, name="xs", tag="xs", align_bytes=64)
                q_tiles[k] = (xq, xs)
                spans = [(0, 512)]
            else:
                xq, xs = q_tiles[k]
                spans = [(512, 1024), (1024, 1280)]
            for a, b in spans:
                nc.vector.quantize_mx(
                    out=xq[:, a:b].bitcast(FP8X4), scales=xs[:, a:b], in_=g[:, 4 * a : 4 * b]
                )

        def mx(acc, xq, xs, col, b, start, stop):
            nc.tensor.matmul_mx(
                out=acc,
                lhsT=xq[:, col : col + P].bitcast(FP8X4),
                lhsT_scale=xs[:, col : col + P],
                rhs=wq[:, b * O : (b + 1) * O].bitcast(FP8X4),
                rhs_scale=wsc[:, b * O : (b + 1) * O],
                start=start,
                stop=stop,
            )

        def passes(s):
            c, t = tiles[s]
            T = CHUNKS[c]
            xq, xs = q_tiles[s // 2]
            q = s % 2
            acc = pso.tile([P, 512], F32, name="acc", tag="o")
            if t == 0:
                c_tiles[c] = psc.tile([P, 512], F32, name="acc4", tag="c")
                o_tiles[c] = opool.tile([P, T * N * O], F32, name="res", tag="res")
            acc4 = c_tiles[c]
            res = o_tiles[c]
            for j in range(N):
                dst = acc[:, j * O : (j + 1) * O] if j < 4 else acc4[:, t * O : (t + 1) * O]
                if j > 0:
                    mx(dst, xq, xs, (j - 1) * 256 + q * P, 5 + j - 1, True, False)
                mx(dst, xq, xs, j * 256 + q * P, j, j == 0, True)
            nc.vector.tensor_tensor(
                out=res[:, t * N * O : t * N * O + 512], in0=acc[:], in1=bias_a[:], op=ADD
            )
            if t == T - 1:
                nc.vector.tensor_tensor(
                    out=res[:].rearrange("p (t c) -> p t c", t=T)[:, :, 512:640],
                    in0=acc4[:, 0 : T * O].rearrange("p (t c) -> p t c", t=T),
                    in1=bias_c[:, 0 : T * O].rearrange("p (t c) -> p t c", t=T),
                    op=ADD,
                )
                r0 = chunk_base[c]
                nc.sync.dma_start(
                    out=out[r0 : r0 + P * T, :].rearrange("(p t) c -> p (t c)", t=T), in_=res[:]
                )

        for s in range(-LEAD, n_tiles):
            if s + LEAD < n_tiles:
                transposes(s + LEAD)
            if 0 <= s + LEAD - 1 < n_tiles:
                quantise(s + LEAD - 1)
            if s >= 0:
                passes(s)
